import numpy as np
import ml_dtypes


def mxq(x, axis, fmt="e4m3"):
    dtype, down = {"e4m3": (ml_dtypes.float8_e4m3fn, 7), "e5m2": (ml_dtypes.float8_e5m2, 14)}[fmt]
    v = np.moveaxis(np.asarray(x, np.float32).astype(ml_dtypes.bfloat16).astype(np.float64), axis, -1)
    blocks = v.reshape(v.shape[:-1] + (-1, 32))
    amax = np.abs(blocks).max(-1, keepdims=True)
    byte = np.maximum(np.where(amax > 0, np.frexp(amax)[1] - 1 + 127, 0) - down, 1)
    scale = np.exp2(byte - 127.0)
    codes = (blocks / scale).astype(np.float32).astype(dtype).astype(np.float64)
    return np.moveaxis((codes * scale).reshape(v.shape), -1, axis)


WIDE = False


def mx_kscale(k):
    if not WIDE:
        return np.ones(k)
    levels = np.array([30, -30])
    if k % 512:
        return np.exp2(np.random.permutation(np.resize(levels, k // 32))).repeat(32)
    a = np.empty((k // 512, 16))
    for p in range(k // 512):
        a[p, :8] = np.random.permutation(np.resize(levels, 8))
        for g in range(8):
            far = levels[np.abs(levels - a[p, g]) >= 10]
            a[p, g + 8] = far[np.random.randint(len(far))]
    return np.exp2(a.ravel()).repeat(32)


BF16 = ml_dtypes.bfloat16


def bf(x):
    return np.asarray(x, np.float32).astype(BF16)


def f64(x):
    return np.asarray(x).astype(np.float64)


B, T, N, C, WIN, F = 1, 4, 512, 512, 3, 3
NW = T - WIN + 1


def sigmoid(v):
    return 1.0 / (1.0 + np.exp(-v))


def setup_inputs():
    t = mx_kscale(C)
    return {"agg": bf(np.random.standard_normal((B, NW, N, C)) * t),
            "W": bf(np.random.standard_normal((NW, F, C, 2 * C)) / np.sqrt(C) / t[:, None]),
            "b": bf(np.random.standard_normal((NW, F, 2 * C)) * 0.3)}


def reference(agg, W, b):
    pre = (mxq(f64(agg), 3, "e5m2")[:, :, None] @ mxq(f64(W), 2, "e5m2")) + f64(b)[None, :, :, None, :]
    lhs, rhs = pre[..., :C], pre[..., C:]
    glu = lhs * sigmoid(rhs)
    return glu.max(axis=2)

@@ -1,0 +1,294 @@
+from contextlib import ExitStack
+
+import concourse.mybir as mybir
+from concourse.masks import make_identity
+
+NW, NF, NODES, C = 2, 3, 512, 512
+FLOPS = 2 * NW * NF * NODES * C * 2 * C
+
+F32 = mybir.dt.float32
+BF16 = mybir.dt.bfloat16
+U32 = mybir.dt.uint32
+U8 = mybir.dt.uint8
+E5M2X4 = mybir.dt.float8_e5m2_x4
+ALU = mybir.AluOpType
+ACT = mybir.ActivationFunctionType
+
+P = 128
+PACK = 4
+PAIR = 2 * P
+STEPS = [(0, q, f) for f in range(NF) for q in range(2)] + [(1, q, f) for q in range(2) for f in range(NF)]
+AGG_STEPS = (2, 3)
+AGG_Q = 4
+GB = 2
+PROD_FIRST = 2
+FIRST = 'q'
+AGG1_AFTER=1
+WFIRST=0
+AGGV=0
+SPOS=0
+LS=2
+LG=2
+LV=2
+HEAD4=1
+TAIL=1
+ORDER=0
+GH = 0
+RULE=None
+OFF=()
+TAILSPLIT=0
+
+V_SHARE = [160, 208, 208, 208, 240, 80, 0, 48, 48, 208, 48, 48]
+G_SHARE = [0] * 12
+
+
+def tile_stsindividuallayer_pb_kernel(tc, agg, W, b, out):
+    nc = tc.nc
+    n_steps = len(STEPS)
+
+    with ExitStack() as ctx:
+        keep = ctx.enter_context(tc.tile_pool(name="keep", bufs=1))
+        work = ctx.enter_context(tc.tile_pool(name="work", bufs=2))
+        psum = ctx.enter_context(tc.psum_pool(name="psum", bufs=1))
+        ctx.enter_context(tc.manual_schedule())
+
+        ident = keep.tile([P, P], F32, name="ident")
+        bias_rows = keep.tile([NW * NF * 8, P], BF16, name="bias_rows")
+        bias_square = keep.tile([P, P], F32, name="bias_square")
+        bias = keep.tile([P, NW * NF * 8], F32, name="bias")
+        agg_raw = [keep.tile([P, PACK, C], BF16, name="agg_raw%d" % w) for w in range(NW)]
+        agg_grouped = [keep.tile([P, NODES, PACK], BF16, name="agg_grouped%d" % w, align_bytes=64) for w in range(NW)]
+        agg_codes = [keep.tile([P, NODES], U32, name="agg_codes%d" % w, align_bytes=64) for w in range(NW)]
+        agg_scales = [keep.tile([P, NODES], U8, name="agg_scales%d" % w, align_bytes=64) for w in range(NW)]
+        w_raw = [keep.tile([P, 2 * PACK, C], BF16, name="w_raw%d" % i) for i in range(n_steps // 2)]
+        best = [keep.tile([P, PACK, C], F32, name="best%d" % w) for w in range(NW)]
+        w_grouped, w_codes, w_scales, lin, gate, sig, glu, flipped = {}, {}, {}, {}, {}, {}, {}, {}
+
+        lb = {}
+
+        def load_agg(w, half):
+            rows = agg[0, w].rearrange("(p t) k -> p t k", t=PACK)
+            nc.sync.dma_start(out=agg_raw[w][:, 2 * half : 2 * half + 2, :], in_=rows[:, 2 * half : 2 * half + 2, :])
+
+        def load_w(br, part=None):
+            w, f = divmod(br, NF)
+            rows = W[w, f].rearrange("k (h x) -> (k h) x", h=2).rearrange("(p r) x -> p r x", r=2 * PACK)
+            if part is None:
+                nc.sync.dma_start(out=w_raw[br][:], in_=rows)
+            elif FIRST == 'q':
+                nc.sync.dma_start(out=w_raw[br][:, :, part * PAIR : (part + 1) * PAIR], in_=rows[:, :, part * PAIR : (part + 1) * PAIR])
+            else:
+                nc.sync.dma_start(out=w_raw[br][:, part::2, :], in_=rows[:, part::2, :])
+
+        def transpose_agg(w, half):
+            words = agg_raw[w][:].rearrange("p t k -> p (t k)").bitcast(F32)
+            bank = psum.tile([P, 2, 2, P], F32, name="agg_bank", tag="flip", bufs=3)
+            for tt in range(2):
+                t = 2 * half + tt
+                for u in range(2):
+                    nc.tensor.transpose(bank[:, tt, u, :], words[:, t * 256 + u : (t + 1) * 256 : 2], ident[:])
+            return bank
+
+        def copy_agg(w, half, bank):
+            dst = agg_grouped[w][:].rearrange("p m j -> p (m j)").bitcast(F32)[:, half * 512 : (half + 1) * 512]
+            nc.scalar.copy(
+                out=dst.rearrange("p (t r u) -> p t r u", t=2, u=2),
+                in_=bank[:].rearrange("p t u r -> p t r u"),
+            )
+
+        def quantize_agg(w):
+            nc.vector.quantize_mx(
+                out=agg_codes[w][:].bitcast(E5M2X4),
+                scales=agg_scales[w][:],
+                in_=agg_grouped[w][:].rearrange("p m j -> p (m j)"),
+            )
+
+        def interleave_views(i, c0, c1):
+            if i not in w_grouped:
+                w_grouped[i] = work.tile([P, 2, PAIR, PACK], BF16, name="w_grouped", bufs=GB, align_bytes=64)
+            w, q, f = STEPS[i]
+            src = w_raw[w * NF + f][:].rearrange("p (j h) c -> p h j c", h=2)[:, :, :, q * PAIR + c0 : q * PAIR + c1]
+            return w_grouped[i][:, :, c0:c1, :], src
+
+        def interleave_vector(i):
+            if V_SHARE[i] > 0:
+                dst, src = interleave_views(i, 0, V_SHARE[i])
+                nc.vector.tensor_copy(
+                    out=dst.rearrange("p h (c i) j -> p h c j i", i=4), in_=src.rearrange("p h j (c i) -> p h c j i", i=4)
+                )
+
+        def interleave_gpsimd(i):
+            if G_SHARE[i] > 0:
+                dst, src = interleave_views(i, V_SHARE[i], V_SHARE[i] + G_SHARE[i])
+                nc.gpsimd.tensor_scalar(
+                    out=dst, in0=src.rearrange("p h j c -> p h c j"), scalar1=1.0, scalar2=0.0, op0=ALU.mult, op1=ALU.add
+                )
+
+        def interleave_scalar(i):
+            if V_SHARE[i] + G_SHARE[i] < PAIR:
+                dst, src = interleave_views(i, V_SHARE[i] + G_SHARE[i], PAIR)
+                nc.scalar.copy(
+                    out=dst.rearrange("p h (c i) j -> p h c j i", i=4), in_=src.rearrange("p h j (c i) -> p h c j i", i=4)
+                )
+
+        def quantize_w(i):
+            w_codes[i] = work.tile([P, 2 * PAIR], U32, name="w_codes", bufs=3, align_bytes=64)
+            w_scales[i] = work.tile([P, 2 * PAIR], U8, name="w_scales", bufs=3, align_bytes=64)
+            nc.vector.quantize_mx(
+                out=w_codes[i][:].bitcast(E5M2X4),
+                scales=w_scales[i][:],
+                in_=w_grouped[i][:].rearrange("p h c j -> p (h c j)"),
+            )
+
+        def multiply(i):
+            w = STEPS[i][0]
+            for a in range(2):
+                gate[i, a] = psum.tile([P, NODES], F32, name="gate", bufs=2)
+                lin[i, a] = psum.tile([P, NODES], F32, name="lin", bufs=3)
+                for h, bank in ((1, gate[i, a]), (0, lin[i, a])):
+                    cols = slice(h * PAIR + a * P, h * PAIR + (a + 1) * P)
+                    nc.tensor.matmul_mx(
+                        out=bank[:],
+                        lhsT=w_codes[i][:, cols].bitcast(E5M2X4),
+                        lhsT_scale=w_scales[i][:, cols],
+                        rhs=agg_codes[w][:].bitcast(E5M2X4),
+                        rhs_scale=agg_scales[w][:],
+                        start=True,
+                        stop=True,
+                    )
+
+        def bias_column(i, h, a):
+            w, q, f = STEPS[i]
+            col = (w * NF + f) * 8 + h * 4 + 2 * q + a
+            return bias[:, col : col + 1]
+
+        def sigmoid(i, a):
+            sig[i, a] = work.tile([P, NODES], F32, name="sig", bufs=4)
+            nc.scalar.activation(out=sig[i, a][:], in_=gate[i, a][:], func=ACT.Sigmoid, bias=bias_column(i, 1, a))
+            if (i, a) in OFF:
+                lb[i, a] = work.tile([P, NODES], F32, name="lb", bufs=3)
+                nc.scalar.activation(out=lb[i, a][:], in_=lin[i, a][:], func=ACT.Identity, bias=bias_column(i, 0, a))
+
+        def product(i, a):
+            glu[i, a] = work.tile([P, NODES], F32, name="glu", bufs=4)
+            if (i, a) in OFF:
+                nc.gpsimd.tensor_tensor(out=glu[i, a][:], in0=lb[i, a][:], in1=sig[i, a][:], op=ALU.mult)
+                return
+            nc.vector.scalar_tensor_tensor(
+                out=glu[i, a][:], in0=lin[i, a][:], scalar=bias_column(i, 0, a), in1=sig[i, a][:], op0=ALU.add, op1=ALU.mult
+            )
+
+        def flip(i):
+            for a in range(2):
+                flipped[i, a] = psum.tile([P, PACK, P], F32, name="flipped", tag="flip", bufs=3)
+                for t in range(PACK):
+                    nc.tensor.transpose(flipped[i, a][:, t, :], glu[i, a][:, t * P : (t + 1) * P], ident[:])
+
+        def merge(i, a):
+            w, q, f = STEPS[i]
+            dst = best[w][:, :, q * PAIR + a * P : q * PAIR + (a + 1) * P]
+            if f == 0:
+                nc.scalar.copy(out=dst, in_=flipped[i, a][:])
+            else:
+                nc.vector.tensor_tensor(out=dst, in0=flipped[i, a][:], in1=dst, op=ALU.max)
+
+        def store(i, c0, c1):
+            w, q, f = STEPS[i]
+            rows = out[0, w].rearrange("(p t) c -> p t c", t=PACK)
+            nc.sync.dma_start(out=rows[:, :, q * PAIR + c0 : q * PAIR + c1], in_=best[w][:, :, q * PAIR + c0 : q * PAIR + c1])
+
+        bias_hbm = b.rearrange("w f (g c) -> (w f g) c", c=P)
+        if WFIRST:
+            load_w(0, 0)
+        load_agg(0, 0)
+        load_agg(0, 1)
+        nc.sync.dma_start(out=bias_rows[0:32, :], in_=bias_hbm[0:32, :])
+        nc.sync.dma_start(out=bias_rows[32:48, :], in_=bias_hbm[32:48, :])
+        if FIRST == 'w':
+            load_w(0)
+        else:
+            if not WFIRST:
+                load_w(0, 0)
+            load_w(0, 1)
+        for br in range(1, NW * NF):
+            load_w(br)
+            if br == AGG1_AFTER:
+                load_agg(1, 0)
+                load_agg(1, 1)
+
+        make_identity(nc, ident[:])
+        nc.gpsimd.memset(bias_square[:], 0.0)
+        nc.gpsimd.tensor_copy(out=bias_square[0 : NW * NF * 8, :], in_=bias_rows[:])
+        words = agg_raw[0][:].rearrange("p t k -> p (t k)").bitcast(F32)
+        gw = agg_grouped[0][:].rearrange("p m j -> p (m j)").bitcast(F32)
+        for t in range(4):
+            bank = psum.tile([P, 2, P], F32, name="agg0_bank", tag="flip" if t % 2 == 0 else "lin", bufs=3)
+            for u in range(2):
+                nc.tensor.transpose(bank[:, u, :], words[:, t * 256 + u : (t + 1) * 256 : 2], ident[:])
+            dst = gw[:, t * 256 : (t + 1) * 256].rearrange("p (r u) -> p r u", u=2)
+            if t % 2 == 0:
+                nc.scalar.copy(out=dst, in_=bank[:].rearrange("p u r -> p r u"))
+            else:
+                nc.vector.tensor_copy(out=dst, in_=bank[:].rearrange("p u r -> p r u"))
+        bias_bank = psum.tile([P, P], F32, name="bias_bank", tag="flip", bufs=3)
+        nc.tensor.transpose(bias_bank[:], bias_square[:], ident[:])
+        nc.scalar.copy(out=bias[:], in_=bias_bank[:, 0 : NW * NF * 8])
+        done = {"v": 0, "s": 0, "g": 0}
+
+        def upto(kind, j):
+            while done[kind] <= min(j, n_steps - 1):
+                {"v": interleave_vector, "s": interleave_scalar, "g": interleave_gpsimd}[kind](done[kind])
+                done[kind] += 1
+
+        upto("s", 0)
+        upto("g", 0)
+        if GH:
+            quantize_agg(0)
+            upto("v", 0)
+        else:
+            upto("v", 0)
+            quantize_agg(0)
+        quantize_w(0)
+        multiply(0)
+        upto("v", LV - 1)
+        upto("g", LG - 1)
+        upto("s", 1)
+        sigmoid(0, 0)
+        sigmoid(0, 1)
+        upto("s", LS - 1)
+
+        for i in range(n_steps + 1):
+            if i >= 1:
+                flip(i - 1)
+            agg_bank = transpose_agg(1, AGG_STEPS.index(i)) if i in AGG_STEPS else None
+            if i + 1 < n_steps:
+                quantize_w(i + 1)
+                multiply(i + 1)
+            upto("v", i + LV)
+            upto("g", i + LG)
+            if SPOS == 0:
+                upto("s", i + LS)
+            if i == AGG_Q:
+                quantize_agg(1)
+            pf = PROD_FIRST == 1 or (PROD_FIRST == 2 and i == n_steps - 1)
+            if pf and i < n_steps:
+                product(i, 0)
+                product(i, 1)
+            for a in range(2):
+                if i >= 1:
+                    merge(i - 1, a)
+                    if i == n_steps:
+                        store(i - 1, a * P, (a + 1) * P)
+                if i < n_steps and not pf:
+                    product(i, a)
+            if 1 <= i < n_steps and STEPS[i - 1][2] == NF - 1:
+                store(i - 1, 0, PAIR)
+            if SPOS == 2:
+                upto("s", i + LS)
+            if agg_bank is not None:
+                copy_agg(1, AGG_STEPS.index(i), agg_bank)
+            if i + 1 < n_steps:
+                sigmoid(i + 1, 0)
+                sigmoid(i + 1, 1)
+            if SPOS == 1:
+                upto("s", i + LS)

@@ -16,35 +16,46 @@ ACT = mybir.ActivationFunctionType
 
 P = 128
 PACK = 4
+LIN, GATE = 0, 1
 PAIR = 2 * P
-STEPS = [(0, q, f) for f in range(NF) for q in range(2)] + [(1, q, f) for q in range(2) for f in range(NF)]
-AGG_STEPS = (2, 3)
-AGG_Q = 4
-GB = 2
-PROD_FIRST = 2
-FIRST = 'q'
-AGG1_AFTER=1
-WFIRST=0
-AGGV=0
-SPOS=0
-LS=2
-LG=2
-LV=2
-HEAD4=1
-TAIL=1
-ORDER=0
-GH = 0
-RULE=None
-OFF=()
-TAILSPLIT=0
+BIAS_ROWS = NW * NF * 2 * C // P
 
-V_SHARE = [160, 208, 208, 208, 240, 80, 0, 48, 48, 208, 48, 48]
-G_SHARE = [0] * 12
+STEPS = [(0, q, f) for f in range(NF) for q in range(2)] + [(1, q, f) for q in range(2) for f in range(NF)]
+LAST = len(STEPS) - 1
+AGG1_TRANSPOSE_STEPS = (1, 3)
+AGG1_QUANTIZE_STEP = 4
+
+VECTOR_FIRST = 144
+VECTOR_EARLY = 224
+VECTOR_NO_MAX = 128
+VECTOR_AGG_EXTRA = 64
+GPSIMD_SHORT = 48
+GPSIMD_LONG = 112
+
+
+def merges_on_vector(step):
+    return step >= 1 and STEPS[step - 1][2] > 0
+
+
+def vector_share(i):
+    if i == 0:
+        return VECTOR_FIRST
+    if i <= 2:
+        return VECTOR_EARLY
+    if i - 2 == AGG1_QUANTIZE_STEP:
+        return 0
+    share = 0 if merges_on_vector(i - 2) else VECTOR_NO_MAX
+    return share + (VECTOR_AGG_EXTRA if i - 2 in AGG1_TRANSPOSE_STEPS else 0)
+
+
+def gpsimd_share(i):
+    if i <= 2:
+        return 0
+    return GPSIMD_LONG if merges_on_vector(i - 3) else GPSIMD_SHORT
 
 
 def tile_stsindividuallayer_pb_kernel(tc, agg, W, b, out):
     nc = tc.nc
-    n_steps = len(STEPS)
 
     with ExitStack() as ctx:
         keep = ctx.enter_context(tc.tile_pool(name="keep", bufs=1))
@@ -53,242 +64,217 @@ def tile_stsindividuallayer_pb_kernel(tc, agg, W, b, out):
         ctx.enter_context(tc.manual_schedule())
 
         ident = keep.tile([P, P], F32, name="ident")
-        bias_rows = keep.tile([NW * NF * 8, P], BF16, name="bias_rows")
+        bias_rows = keep.tile([BIAS_ROWS, P], BF16, name="bias_rows")
         bias_square = keep.tile([P, P], F32, name="bias_square")
-        bias = keep.tile([P, NW * NF * 8], F32, name="bias")
+        bias = keep.tile([P, BIAS_ROWS], F32, name="bias")
         agg_raw = [keep.tile([P, PACK, C], BF16, name="agg_raw%d" % w) for w in range(NW)]
-        agg_grouped = [keep.tile([P, NODES, PACK], BF16, name="agg_grouped%d" % w, align_bytes=64) for w in range(NW)]
+        agg_grouped = [keep.tile([P, NODES * PACK], BF16, name="agg_grouped%d" % w, align_bytes=64) for w in range(NW)]
         agg_codes = [keep.tile([P, NODES], U32, name="agg_codes%d" % w, align_bytes=64) for w in range(NW)]
         agg_scales = [keep.tile([P, NODES], U8, name="agg_scales%d" % w, align_bytes=64) for w in range(NW)]
-        w_raw = [keep.tile([P, 2 * PACK, C], BF16, name="w_raw%d" % i) for i in range(n_steps // 2)]
+        w_raw = [keep.tile([P, 2 * PACK, C], BF16, name="w_raw%d" % i) for i in range(NW * NF)]
         best = [keep.tile([P, PACK, C], F32, name="best%d" % w) for w in range(NW)]
-        w_grouped, w_codes, w_scales, lin, gate, sig, glu, flipped = {}, {}, {}, {}, {}, {}, {}, {}
+        w_grouped, w_codes, w_scales, pre, sig, glu, flipped = {}, {}, {}, {}, {}, {}, {}
 
-        lb = {}
+        def flip_bank(shape):
+            return psum.tile(shape, F32, name="flip", bufs=3)
 
-        def load_agg(w, half):
+        def pre_bank(half, shape):
+            if half == GATE:
+                return psum.tile(shape, F32, name="gate", bufs=2)
+            return psum.tile(shape, F32, name="lin", bufs=3)
+
+        def load_agg(w):
             rows = agg[0, w].rearrange("(p t) k -> p t k", t=PACK)
-            nc.sync.dma_start(out=agg_raw[w][:, 2 * half : 2 * half + 2, :], in_=rows[:, 2 * half : 2 * half + 2, :])
+            for t0 in (0, 2):
+                nc.sync.dma_start(out=agg_raw[w][:, t0 : t0 + 2, :], in_=rows[:, t0 : t0 + 2, :])
 
-        def load_w(br, part=None):
-            w, f = divmod(br, NF)
+        def load_w(w, f, cols):
             rows = W[w, f].rearrange("k (h x) -> (k h) x", h=2).rearrange("(p r) x -> p r x", r=2 * PACK)
-            if part is None:
-                nc.sync.dma_start(out=w_raw[br][:], in_=rows)
-            elif FIRST == 'q':
-                nc.sync.dma_start(out=w_raw[br][:, :, part * PAIR : (part + 1) * PAIR], in_=rows[:, :, part * PAIR : (part + 1) * PAIR])
-            else:
-                nc.sync.dma_start(out=w_raw[br][:, part::2, :], in_=rows[:, part::2, :])
+            nc.sync.dma_start(out=w_raw[w * NF + f][:, :, cols], in_=rows[:, :, cols])
 
-        def transpose_agg(w, half):
-            words = agg_raw[w][:].rearrange("p t k -> p (t k)").bitcast(F32)
-            bank = psum.tile([P, 2, 2, P], F32, name="agg_bank", tag="flip", bufs=3)
-            for tt in range(2):
-                t = 2 * half + tt
-                for u in range(2):
-                    nc.tensor.transpose(bank[:, tt, u, :], words[:, t * 256 + u : (t + 1) * 256 : 2], ident[:])
-            return bank
+        def transpose_agg(w, t, bank):
+            words = agg_raw[w][:, t, :].bitcast(F32)
+            for u in range(2):
+                nc.tensor.transpose(bank[:, u, :], words[:, u : C // 2 : 2], ident[:])
 
-        def copy_agg(w, half, bank):
-            dst = agg_grouped[w][:].rearrange("p m j -> p (m j)").bitcast(F32)[:, half * 512 : (half + 1) * 512]
-            nc.scalar.copy(
-                out=dst.rearrange("p (t r u) -> p t r u", t=2, u=2),
-                in_=bank[:].rearrange("p t u r -> p t r u"),
-            )
+        def agg_words(w, t0, t1):
+            words = agg_grouped[w][:].bitcast(F32)
+            return words[:, t0 * 2 * P : t1 * 2 * P].rearrange("p (t r u) -> p t r u", r=P, u=2)
 
         def quantize_agg(w):
-            nc.vector.quantize_mx(
-                out=agg_codes[w][:].bitcast(E5M2X4),
-                scales=agg_scales[w][:],
-                in_=agg_grouped[w][:].rearrange("p m j -> p (m j)"),
-            )
+            nc.vector.quantize_mx(out=agg_codes[w][:].bitcast(E5M2X4), scales=agg_scales[w][:], in_=agg_grouped[w][:])
 
-        def interleave_views(i, c0, c1):
-            if i not in w_grouped:
-                w_grouped[i] = work.tile([P, 2, PAIR, PACK], BF16, name="w_grouped", bufs=GB, align_bytes=64)
+        def interleave(i):
             w, q, f = STEPS[i]
-            src = w_raw[w * NF + f][:].rearrange("p (j h) c -> p h j c", h=2)[:, :, :, q * PAIR + c0 : q * PAIR + c1]
-            return w_grouped[i][:, :, c0:c1, :], src
+            w_grouped[i] = work.tile([P, 2, PAIR, PACK], BF16, name="w_grouped", bufs=2, align_bytes=64)
+            raw = w_raw[w * NF + f][:].rearrange("p (j h) x -> p h j x", h=2)[:, :, :, q * PAIR : (q + 1) * PAIR]
+            v_end = vector_share(i)
+            g_end = v_end + gpsimd_share(i)
 
-        def interleave_vector(i):
-            if V_SHARE[i] > 0:
-                dst, src = interleave_views(i, 0, V_SHARE[i])
-                nc.vector.tensor_copy(
-                    out=dst.rearrange("p h (c i) j -> p h c j i", i=4), in_=src.rearrange("p h j (c i) -> p h c j i", i=4)
+            def by_fours(c0, c1):
+                return dict(
+                    out=w_grouped[i][:, :, c0:c1, :].rearrange("p h (c i) j -> p h c j i", i=4),
+                    in_=raw[:, :, :, c0:c1].rearrange("p h j (c i) -> p h c j i", i=4),
                 )
 
-        def interleave_gpsimd(i):
-            if G_SHARE[i] > 0:
-                dst, src = interleave_views(i, V_SHARE[i], V_SHARE[i] + G_SHARE[i])
+            if v_end > 0:
+                nc.vector.tensor_copy(**by_fours(0, v_end))
+            if g_end > v_end:
                 nc.gpsimd.tensor_scalar(
-                    out=dst, in0=src.rearrange("p h j c -> p h c j"), scalar1=1.0, scalar2=0.0, op0=ALU.mult, op1=ALU.add
+                    out=w_grouped[i][:, :, v_end:g_end, :],
+                    in0=raw[:, :, :, v_end:g_end].rearrange("p h j c -> p h c j"),
+                    scalar1=1.0,
+                    scalar2=0.0,
+                    op0=ALU.mult,
+                    op1=ALU.add,
                 )
-
-        def interleave_scalar(i):
-            if V_SHARE[i] + G_SHARE[i] < PAIR:
-                dst, src = interleave_views(i, V_SHARE[i] + G_SHARE[i], PAIR)
-                nc.scalar.copy(
-                    out=dst.rearrange("p h (c i) j -> p h c j i", i=4), in_=src.rearrange("p h j (c i) -> p h c j i", i=4)
-                )
+            nc.scalar.copy(**by_fours(g_end, PAIR))
 
         def quantize_w(i):
-            w_codes[i] = work.tile([P, 2 * PAIR], U32, name="w_codes", bufs=3, align_bytes=64)
-            w_scales[i] = work.tile([P, 2 * PAIR], U8, name="w_scales", bufs=3, align_bytes=64)
+            w_codes[i] = work.tile([P, 2 * PAIR], U32, name="w_codes", bufs=4, align_bytes=64)
+            w_scales[i] = work.tile([P, 2 * PAIR], U8, name="w_scales", bufs=4, align_bytes=64)
             nc.vector.quantize_mx(
                 out=w_codes[i][:].bitcast(E5M2X4),
                 scales=w_scales[i][:],
                 in_=w_grouped[i][:].rearrange("p h c j -> p (h c j)"),
             )
 
-        def multiply(i):
+        def multiply(i, half, a):
             w = STEPS[i][0]
-            for a in range(2):
-                gate[i, a] = psum.tile([P, NODES], F32, name="gate", bufs=2)
-                lin[i, a] = psum.tile([P, NODES], F32, name="lin", bufs=3)
-                for h, bank in ((1, gate[i, a]), (0, lin[i, a])):
-                    cols = slice(h * PAIR + a * P, h * PAIR + (a + 1) * P)
-                    nc.tensor.matmul_mx(
-                        out=bank[:],
-                        lhsT=w_codes[i][:, cols].bitcast(E5M2X4),
-                        lhsT_scale=w_scales[i][:, cols],
-                        rhs=agg_codes[w][:].bitcast(E5M2X4),
-                        rhs_scale=agg_scales[w][:],
-                        start=True,
-                        stop=True,
-                    )
+            pre[i, half, a] = pre_bank(half, [P, NODES])
+            cols = slice(half * PAIR + a * P, half * PAIR + (a + 1) * P)
+            nc.tensor.matmul_mx(
+                out=pre[i, half, a][:],
+                lhsT=w_codes[i][:, cols].bitcast(E5M2X4),
+                lhsT_scale=w_scales[i][:, cols],
+                rhs=agg_codes[w][:].bitcast(E5M2X4),
+                rhs_scale=agg_scales[w][:],
+                start=True,
+                stop=True,
+            )
 
-        def bias_column(i, h, a):
+        def bias_column(i, half, a):
             w, q, f = STEPS[i]
-            col = (w * NF + f) * 8 + h * 4 + 2 * q + a
-            return bias[:, col : col + 1]
+            row = ((w * NF + f) * 2 * C + half * C + q * PAIR + a * P) // P
+            return bias[:, row : row + 1]
 
-        def sigmoid(i, a):
-            sig[i, a] = work.tile([P, NODES], F32, name="sig", bufs=4)
-            nc.scalar.activation(out=sig[i, a][:], in_=gate[i, a][:], func=ACT.Sigmoid, bias=bias_column(i, 1, a))
-            if (i, a) in OFF:
-                lb[i, a] = work.tile([P, NODES], F32, name="lb", bufs=3)
-                nc.scalar.activation(out=lb[i, a][:], in_=lin[i, a][:], func=ACT.Identity, bias=bias_column(i, 0, a))
+        def sigmoids(i):
+            for a in range(2):
+                sig[i, a] = work.tile([P, NODES], F32, name="sig", bufs=6)
+                nc.scalar.activation(
+                    out=sig[i, a][:], in_=pre[i, GATE, a][:], func=ACT.Sigmoid, bias=bias_column(i, GATE, a)
+                )
 
         def product(i, a):
             glu[i, a] = work.tile([P, NODES], F32, name="glu", bufs=4)
-            if (i, a) in OFF:
-                nc.gpsimd.tensor_tensor(out=glu[i, a][:], in0=lb[i, a][:], in1=sig[i, a][:], op=ALU.mult)
-                return
             nc.vector.scalar_tensor_tensor(
-                out=glu[i, a][:], in0=lin[i, a][:], scalar=bias_column(i, 0, a), in1=sig[i, a][:], op0=ALU.add, op1=ALU.mult
+                out=glu[i, a][:],
+                in0=pre[i, LIN, a][:],
+                scalar=bias_column(i, LIN, a),
+                in1=sig[i, a][:],
+                op0=ALU.add,
+                op1=ALU.mult,
             )
 
-        def flip(i):
-            for a in range(2):
-                flipped[i, a] = psum.tile([P, PACK, P], F32, name="flipped", tag="flip", bufs=3)
-                for t in range(PACK):
-                    nc.tensor.transpose(flipped[i, a][:, t, :], glu[i, a][:, t * P : (t + 1) * P], ident[:])
+        def flip(i, a):
+            flipped[i, a] = flip_bank([P, PACK, P])
+            for t in range(PACK):
+                nc.tensor.transpose(flipped[i, a][:, t, :], glu[i, a][:, t * P : (t + 1) * P], ident[:])
 
-        def merge(i, a):
+        def channels(i, a0, a1):
+            q = STEPS[i][1]
+            return slice(q * PAIR + a0 * P, q * PAIR + a1 * P)
+
+        def merge(i, a, ts=slice(0, PACK)):
             w, q, f = STEPS[i]
-            dst = best[w][:, :, q * PAIR + a * P : q * PAIR + (a + 1) * P]
+            dst = best[w][:, ts, channels(i, a, a + 1)]
             if f == 0:
-                nc.scalar.copy(out=dst, in_=flipped[i, a][:])
+                nc.scalar.copy(out=dst, in_=flipped[i, a][:, ts, :])
             else:
-                nc.vector.tensor_tensor(out=dst, in0=flipped[i, a][:], in1=dst, op=ALU.max)
+                nc.vector.tensor_tensor(out=dst, in0=flipped[i, a][:, ts, :], in1=dst, op=ALU.max)
 
-        def store(i, c0, c1):
-            w, q, f = STEPS[i]
+        def store(i, a0, a1, ts=slice(0, PACK)):
+            w = STEPS[i][0]
             rows = out[0, w].rearrange("(p t) c -> p t c", t=PACK)
-            nc.sync.dma_start(out=rows[:, :, q * PAIR + c0 : q * PAIR + c1], in_=best[w][:, :, q * PAIR + c0 : q * PAIR + c1])
+            nc.sync.dma_start(out=rows[:, ts, channels(i, a0, a1)], in_=best[w][:, ts, channels(i, a0, a1)])
 
         bias_hbm = b.rearrange("w f (g c) -> (w f g) c", c=P)
-        if WFIRST:
-            load_w(0, 0)
-        load_agg(0, 0)
-        load_agg(0, 1)
+        load_agg(0)
         nc.sync.dma_start(out=bias_rows[0:32, :], in_=bias_hbm[0:32, :])
-        nc.sync.dma_start(out=bias_rows[32:48, :], in_=bias_hbm[32:48, :])
-        if FIRST == 'w':
-            load_w(0)
-        else:
-            if not WFIRST:
-                load_w(0, 0)
-            load_w(0, 1)
-        for br in range(1, NW * NF):
-            load_w(br)
-            if br == AGG1_AFTER:
-                load_agg(1, 0)
-                load_agg(1, 1)
+        nc.sync.dma_start(out=bias_rows[32:BIAS_ROWS, :], in_=bias_hbm[32:BIAS_ROWS, :])
+        load_w(0, 0, slice(0, PAIR))
+        load_w(0, 0, slice(PAIR, C))
+        load_w(0, 1, slice(0, C))
+        load_agg(1)
+        load_w(0, 2, slice(0, C))
+        for f in range(NF):
+            load_w(1, f, slice(0, C))
 
         make_identity(nc, ident[:])
         nc.gpsimd.memset(bias_square[:], 0.0)
-        nc.gpsimd.tensor_copy(out=bias_square[0 : NW * NF * 8, :], in_=bias_rows[:])
-        words = agg_raw[0][:].rearrange("p t k -> p (t k)").bitcast(F32)
-        gw = agg_grouped[0][:].rearrange("p m j -> p (m j)").bitcast(F32)
-        for t in range(4):
-            bank = psum.tile([P, 2, P], F32, name="agg0_bank", tag="flip" if t % 2 == 0 else "lin", bufs=3)
-            for u in range(2):
-                nc.tensor.transpose(bank[:, u, :], words[:, t * 256 + u : (t + 1) * 256 : 2], ident[:])
-            dst = gw[:, t * 256 : (t + 1) * 256].rearrange("p (r u) -> p r u", u=2)
-            if t % 2 == 0:
-                nc.scalar.copy(out=dst, in_=bank[:].rearrange("p u r -> p r u"))
-            else:
-                nc.vector.tensor_copy(out=dst, in_=bank[:].rearrange("p u r -> p r u"))
-        bias_bank = psum.tile([P, P], F32, name="bias_bank", tag="flip", bufs=3)
+        nc.gpsimd.tensor_copy(out=bias_square[0:BIAS_ROWS, :], in_=bias_rows[:])
+        for t in range(PACK):
+            bank = flip_bank([P, 2, P]) if t % 2 == 0 else pre_bank(LIN, [P, 2, P])
+            transpose_agg(0, t, bank)
+            copy = nc.scalar.copy if t % 2 == 0 else nc.vector.tensor_copy
+            copy(out=agg_words(0, t, t + 1)[:, 0], in_=bank[:].rearrange("p u r -> p r u"))
+        bias_bank = flip_bank([P, P])
         nc.tensor.transpose(bias_bank[:], bias_square[:], ident[:])
-        nc.scalar.copy(out=bias[:], in_=bias_bank[:, 0 : NW * NF * 8])
-        done = {"v": 0, "s": 0, "g": 0}
-
-        def upto(kind, j):
-            while done[kind] <= min(j, n_steps - 1):
-                {"v": interleave_vector, "s": interleave_scalar, "g": interleave_gpsimd}[kind](done[kind])
-                done[kind] += 1
-
-        upto("s", 0)
-        upto("g", 0)
-        if GH:
-            quantize_agg(0)
-            upto("v", 0)
-        else:
-            upto("v", 0)
-            quantize_agg(0)
+        nc.scalar.copy(out=bias[:], in_=bias_bank[:, 0:BIAS_ROWS])
+        interleave(0)
+        quantize_agg(0)
         quantize_w(0)
-        multiply(0)
-        upto("v", LV - 1)
-        upto("g", LG - 1)
-        upto("s", 1)
-        sigmoid(0, 0)
-        sigmoid(0, 1)
-        upto("s", LS - 1)
+        for a in range(2):
+            multiply(0, GATE, a)
+            multiply(0, LIN, a)
+        interleave(1)
+        sigmoids(0)
 
-        for i in range(n_steps + 1):
+        for i in range(LAST):
             if i >= 1:
-                flip(i - 1)
-            agg_bank = transpose_agg(1, AGG_STEPS.index(i)) if i in AGG_STEPS else None
-            if i + 1 < n_steps:
+                flip(i - 1, 0)
+                flip(i - 1, 1)
+            if i in AGG1_TRANSPOSE_STEPS:
+                t0 = 2 * AGG1_TRANSPOSE_STEPS.index(i)
+                agg_bank = flip_bank([P, 2, 2, P])
+                transpose_agg(1, t0, agg_bank[:, 0])
+                transpose_agg(1, t0 + 1, agg_bank[:, 1])
+            if i + 1 < LAST:
                 quantize_w(i + 1)
-                multiply(i + 1)
-            upto("v", i + LV)
-            upto("g", i + LG)
-            if SPOS == 0:
-                upto("s", i + LS)
-            if i == AGG_Q:
+            for a in range(2):
+                if i + 1 < LAST:
+                    multiply(i + 1, GATE, a)
+                multiply(i + 1, LIN, a)
+            if i + 2 <= LAST:
+                interleave(i + 2)
+            if i == AGG1_QUANTIZE_STEP:
                 quantize_agg(1)
-            pf = PROD_FIRST == 1 or (PROD_FIRST == 2 and i == n_steps - 1)
-            if pf and i < n_steps:
-                product(i, 0)
-                product(i, 1)
             for a in range(2):
                 if i >= 1:
                     merge(i - 1, a)
-                    if i == n_steps:
-                        store(i - 1, a * P, (a + 1) * P)
-                if i < n_steps and not pf:
-                    product(i, a)
-            if 1 <= i < n_steps and STEPS[i - 1][2] == NF - 1:
-                store(i - 1, 0, PAIR)
-            if SPOS == 2:
-                upto("s", i + LS)
-            if agg_bank is not None:
-                copy_agg(1, AGG_STEPS.index(i), agg_bank)
-            if i + 1 < n_steps:
-                sigmoid(i + 1, 0)
-                sigmoid(i + 1, 1)
-            if SPOS == 1:
-                upto("s", i + LS)
+                product(i, a)
+                if i + 2 == LAST and a == 0:
+                    quantize_w(LAST)
+            if i >= 1 and STEPS[i - 1][2] == NF - 1:
+                store(i - 1, 0, 2)
+            if i in AGG1_TRANSPOSE_STEPS:
+                nc.scalar.copy(out=agg_words(1, t0, t0 + 2), in_=agg_bank[:].rearrange("p t u r -> p t r u"))
+            if i + 1 < LAST:
+                sigmoids(i + 1)
+            if i + 2 == LAST:
+                multiply(LAST, GATE, 0)
+                multiply(LAST, GATE, 1)
+                sigmoids(LAST)
+
+        flip(LAST - 1, 0)
+        flip(LAST - 1, 1)
+        for a in range(2):
+            product(LAST, a)
+            flip(LAST, a)
+        merge(LAST - 1, 0)
+        merge(LAST, 0)
+        store(LAST, 0, 1)
+        merge(LAST - 1, 1)
+        for t0 in (0, 2):
+            merge(LAST, 1, slice(t0, t0 + 2))
+            store(LAST, 1, 2, slice(t0, t0 + 2))

from contextlib import ExitStack

import concourse.mybir as mybir
from concourse.masks import make_identity

NW, NF, NODES, C = 2, 3, 512, 512
FLOPS = 2 * NW * NF * NODES * C * 2 * C

F32 = mybir.dt.float32
BF16 = mybir.dt.bfloat16
U32 = mybir.dt.uint32
U8 = mybir.dt.uint8
E5M2X4 = mybir.dt.float8_e5m2_x4
ALU = mybir.AluOpType
ACT = mybir.ActivationFunctionType

P = 128
PACK = 4
LIN, GATE = 0, 1
PAIR = 2 * P
BIAS_ROWS = NW * NF * 2 * C // P

STEPS = [(0, q, f) for f in range(NF) for q in range(2)] + [(1, q, f) for q in range(2) for f in range(NF)]
LAST = len(STEPS) - 1
AGG1_TRANSPOSE_STEPS = (1, 3)
AGG1_QUANTIZE_STEP = 4

VECTOR_FIRST = 144
VECTOR_EARLY = 224
VECTOR_NO_MAX = 128
VECTOR_AGG_EXTRA = 64
GPSIMD_SHORT = 48
GPSIMD_LONG = 112


def merges_on_vector(step):
    return step >= 1 and STEPS[step - 1][2] > 0


def vector_share(i):
    if i == 0:
        return VECTOR_FIRST
    if i <= 2:
        return VECTOR_EARLY
    if i - 2 == AGG1_QUANTIZE_STEP:
        return 0
    share = 0 if merges_on_vector(i - 2) else VECTOR_NO_MAX
    return share + (VECTOR_AGG_EXTRA if i - 2 in AGG1_TRANSPOSE_STEPS else 0)


def gpsimd_share(i):
    if i <= 2:
        return 0
    return GPSIMD_LONG if merges_on_vector(i - 3) else GPSIMD_SHORT


def tile_stsindividuallayer_pb_kernel(tc, agg, W, b, out):
    nc = tc.nc

    with ExitStack() as ctx:
        keep = ctx.enter_context(tc.tile_pool(name="keep", bufs=1))
        work = ctx.enter_context(tc.tile_pool(name="work", bufs=2))
        psum = ctx.enter_context(tc.psum_pool(name="psum", bufs=1))
        ctx.enter_context(tc.manual_schedule())

        ident = keep.tile([P, P], F32, name="ident")
        bias_rows = keep.tile([BIAS_ROWS, P], BF16, name="bias_rows")
        bias_square = keep.tile([P, P], F32, name="bias_square")
        bias = keep.tile([P, BIAS_ROWS], F32, name="bias")
        agg_raw = [keep.tile([P, PACK, C], BF16, name="agg_raw%d" % w) for w in range(NW)]
        agg_grouped = [keep.tile([P, NODES * PACK], BF16, name="agg_grouped%d" % w, align_bytes=64) for w in range(NW)]
        agg_codes = [keep.tile([P, NODES], U32, name="agg_codes%d" % w, align_bytes=64) for w in range(NW)]
        agg_scales = [keep.tile([P, NODES], U8, name="agg_scales%d" % w, align_bytes=64) for w in range(NW)]
        w_raw = [keep.tile([P, 2 * PACK, C], BF16, name="w_raw%d" % i) for i in range(NW * NF)]
        best = [keep.tile([P, PACK, C], F32, name="best%d" % w) for w in range(NW)]
        w_grouped, w_codes, w_scales, pre, sig, glu, flipped = {}, {}, {}, {}, {}, {}, {}

        def flip_bank(shape):
            return psum.tile(shape, F32, name="flip", bufs=3)

        def pre_bank(half, shape):
            if half == GATE:
                return psum.tile(shape, F32, name="gate", bufs=2)
            return psum.tile(shape, F32, name="lin", bufs=3)

        def load_agg(w):
            rows = agg[0, w].rearrange("(p t) k -> p t k", t=PACK)
            for t0 in (0, 2):
                nc.sync.dma_start(out=agg_raw[w][:, t0 : t0 + 2, :], in_=rows[:, t0 : t0 + 2, :])

        def load_w(w, f, cols):
            rows = W[w, f].rearrange("k (h x) -> (k h) x", h=2).rearrange("(p r) x -> p r x", r=2 * PACK)
            nc.sync.dma_start(out=w_raw[w * NF + f][:, :, cols], in_=rows[:, :, cols])

        def transpose_agg(w, t, bank):
            words = agg_raw[w][:, t, :].bitcast(F32)
            for u in range(2):
                nc.tensor.transpose(bank[:, u, :], words[:, u : C // 2 : 2], ident[:])

        def agg_words(w, t0, t1):
            words = agg_grouped[w][:].bitcast(F32)
            return words[:, t0 * 2 * P : t1 * 2 * P].rearrange("p (t r u) -> p t r u", r=P, u=2)

        def quantize_agg(w):
            nc.vector.quantize_mx(out=agg_codes[w][:].bitcast(E5M2X4), scales=agg_scales[w][:], in_=agg_grouped[w][:])

        def interleave(i):
            w, q, f = STEPS[i]
            w_grouped[i] = work.tile([P, 2, PAIR, PACK], BF16, name="w_grouped", bufs=2, align_bytes=64)
            raw = w_raw[w * NF + f][:].rearrange("p (j h) x -> p h j x", h=2)[:, :, :, q * PAIR : (q + 1) * PAIR]
            v_end = vector_share(i)
            g_end = v_end + gpsimd_share(i)

            def by_fours(c0, c1):
                return dict(
                    out=w_grouped[i][:, :, c0:c1, :].rearrange("p h (c i) j -> p h c j i", i=4),
                    in_=raw[:, :, :, c0:c1].rearrange("p h j (c i) -> p h c j i", i=4),
                )

            if v_end > 0:
                nc.vector.tensor_copy(**by_fours(0, v_end))
            if g_end > v_end:
                nc.gpsimd.tensor_scalar(
                    out=w_grouped[i][:, :, v_end:g_end, :],
                    in0=raw[:, :, :, v_end:g_end].rearrange("p h j c -> p h c j"),
                    scalar1=1.0,
                    scalar2=0.0,
                    op0=ALU.mult,
                    op1=ALU.add,
                )
            nc.scalar.copy(**by_fours(g_end, PAIR))

        def quantize_w(i):
            w_codes[i] = work.tile([P, 2 * PAIR], U32, name="w_codes", bufs=4, align_bytes=64)
            w_scales[i] = work.tile([P, 2 * PAIR], U8, name="w_scales", bufs=4, align_bytes=64)
            nc.vector.quantize_mx(
                out=w_codes[i][:].bitcast(E5M2X4),
                scales=w_scales[i][:],
                in_=w_grouped[i][:].rearrange("p h c j -> p (h c j)"),
            )

        def multiply(i, half, a):
            w = STEPS[i][0]
            pre[i, half, a] = pre_bank(half, [P, NODES])
            cols = slice(half * PAIR + a * P, half * PAIR + (a + 1) * P)
            nc.tensor.matmul_mx(
                out=pre[i, half, a][:],
                lhsT=w_codes[i][:, cols].bitcast(E5M2X4),
                lhsT_scale=w_scales[i][:, cols],
                rhs=agg_codes[w][:].bitcast(E5M2X4),
                rhs_scale=agg_scales[w][:],
                start=True,
                stop=True,
            )

        def bias_column(i, half, a):
            w, q, f = STEPS[i]
            row = ((w * NF + f) * 2 * C + half * C + q * PAIR + a * P) // P
            return bias[:, row : row + 1]

        def sigmoids(i):
            for a in range(2):
                sig[i, a] = work.tile([P, NODES], F32, name="sig", bufs=6)
                nc.scalar.activation(
                    out=sig[i, a][:], in_=pre[i, GATE, a][:], func=ACT.Sigmoid, bias=bias_column(i, GATE, a)
                )

        def product(i, a):
            glu[i, a] = work.tile([P, NODES], F32, name="glu", bufs=4)
            nc.vector.scalar_tensor_tensor(
                out=glu[i, a][:],
                in0=pre[i, LIN, a][:],
                scalar=bias_column(i, LIN, a),
                in1=sig[i, a][:],
                op0=ALU.add,
                op1=ALU.mult,
            )

        def flip(i, a):
            flipped[i, a] = flip_bank([P, PACK, P])
            for t in range(PACK):
                nc.tensor.transpose(flipped[i, a][:, t, :], glu[i, a][:, t * P : (t + 1) * P], ident[:])

        def channels(i, a0, a1):
            q = STEPS[i][1]
            return slice(q * PAIR + a0 * P, q * PAIR + a1 * P)

        def merge(i, a, ts=slice(0, PACK)):
            w, q, f = STEPS[i]
            dst = best[w][:, ts, channels(i, a, a + 1)]
            if f == 0:
                nc.scalar.copy(out=dst, in_=flipped[i, a][:, ts, :])
            else:
                nc.vector.tensor_tensor(out=dst, in0=flipped[i, a][:, ts, :], in1=dst, op=ALU.max)

        def store(i, a0, a1, ts=slice(0, PACK)):
            w = STEPS[i][0]
            rows = out[0, w].rearrange("(p t) c -> p t c", t=PACK)
            nc.sync.dma_start(out=rows[:, ts, channels(i, a0, a1)], in_=best[w][:, ts, channels(i, a0, a1)])

        bias_hbm = b.rearrange("w f (g c) -> (w f g) c", c=P)
        load_agg(0)
        nc.sync.dma_start(out=bias_rows[0:32, :], in_=bias_hbm[0:32, :])
        nc.sync.dma_start(out=bias_rows[32:BIAS_ROWS, :], in_=bias_hbm[32:BIAS_ROWS, :])
        load_w(0, 0, slice(0, PAIR))
        load_w(0, 0, slice(PAIR, C))
        load_w(0, 1, slice(0, C))
        load_agg(1)
        load_w(0, 2, slice(0, C))
        for f in range(NF):
            load_w(1, f, slice(0, C))

        make_identity(nc, ident[:])
        nc.gpsimd.memset(bias_square[:], 0.0)
        nc.gpsimd.tensor_copy(out=bias_square[0:BIAS_ROWS, :], in_=bias_rows[:])
        for t in range(PACK):
            bank = flip_bank([P, 2, P]) if t % 2 == 0 else pre_bank(LIN, [P, 2, P])
            transpose_agg(0, t, bank)
            copy = nc.scalar.copy if t % 2 == 0 else nc.vector.tensor_copy
            copy(out=agg_words(0, t, t + 1)[:, 0], in_=bank[:].rearrange("p u r -> p r u"))
        bias_bank = flip_bank([P, P])
        nc.tensor.transpose(bias_bank[:], bias_square[:], ident[:])
        nc.scalar.copy(out=bias[:], in_=bias_bank[:, 0:BIAS_ROWS])
        interleave(0)
        quantize_agg(0)
        quantize_w(0)
        for a in range(2):
            multiply(0, GATE, a)
            multiply(0, LIN, a)
        interleave(1)
        sigmoids(0)

        for i in range(LAST):
            if i >= 1:
                flip(i - 1, 0)
                flip(i - 1, 1)
            if i in AGG1_TRANSPOSE_STEPS:
                t0 = 2 * AGG1_TRANSPOSE_STEPS.index(i)
                agg_bank = flip_bank([P, 2, 2, P])
                transpose_agg(1, t0, agg_bank[:, 0])
                transpose_agg(1, t0 + 1, agg_bank[:, 1])
            if i + 1 < LAST:
                quantize_w(i + 1)
            for a in range(2):
                if i + 1 < LAST:
                    multiply(i + 1, GATE, a)
                multiply(i + 1, LIN, a)
            if i + 2 <= LAST:
                interleave(i + 2)
            if i == AGG1_QUANTIZE_STEP:
                quantize_agg(1)
            for a in range(2):
                if i >= 1:
                    merge(i - 1, a)
                product(i, a)
                if i + 2 == LAST and a == 0:
                    quantize_w(LAST)
            if i >= 1 and STEPS[i - 1][2] == NF - 1:
                store(i - 1, 0, 2)
            if i in AGG1_TRANSPOSE_STEPS:
                nc.scalar.copy(out=agg_words(1, t0, t0 + 2), in_=agg_bank[:].rearrange("p t u r -> p t r u"))
            if i + 1 < LAST:
                sigmoids(i + 1)
            if i + 2 == LAST:
                multiply(LAST, GATE, 0)
                multiply(LAST, GATE, 1)
                sigmoids(LAST)

        flip(LAST - 1, 0)
        flip(LAST - 1, 1)
        for a in range(2):
            product(LAST, a)
            flip(LAST, a)
        merge(LAST - 1, 0)
        merge(LAST, 0)
        store(LAST, 0, 1)
        merge(LAST - 1, 1)
        for t0 in (0, 2):
            merge(LAST, 1, slice(t0, t0 + 2))
            store(LAST, 1, 2, slice(t0, t0 + 2))
